import numpy as np
import ml_dtypes


def mxq(x, axis, fmt="e4m3"):
    dtype, down = {"e4m3": (ml_dtypes.float8_e4m3fn, 7), "e5m2": (ml_dtypes.float8_e5m2, 14)}[fmt]
    v = np.moveaxis(np.asarray(x, np.float32).astype(ml_dtypes.bfloat16).astype(np.float64), axis, -1)
    blocks = v.reshape(v.shape[:-1] + (-1, 32))
    amax = np.abs(blocks).max(-1, keepdims=True)
    byte = np.maximum(np.where(amax > 0, np.frexp(amax)[1] - 1 + 127, 0) - down, 1)
    scale = np.exp2(byte - 127.0)
    codes = (blocks / scale).astype(np.float32).astype(dtype).astype(np.float64)
    return np.moveaxis((codes * scale).reshape(v.shape), -1, axis)


WIDE = False


def mx_kscale(k):
    if not WIDE:
        return np.ones(k)
    levels = np.array([10, -10, 5, -5, 0])
    a = np.random.permutation(np.resize(levels, k // 512 * 4)).reshape(k // 512, 4)
    idx = np.arange(k)
    return np.exp2(a[idx // 512, idx % 128 // 32])


BF16 = ml_dtypes.bfloat16


def bf(x):
    return np.asarray(x, np.float32).astype(BF16)


def f64(x):
    return np.asarray(x).astype(np.float64)


B, K, NH, N = 8192, 1024, 512, 128
EPSILON = 0.1


def setup_inputs():
    s = mx_kscale(K)
    g = 1.0 / np.mean(1.0 / s)
    return {"x": bf(np.random.standard_normal((B, K)) * s),
            "y": bf(np.random.standard_normal((B, N)) * 12.0 / np.sqrt(K) * g),
            "beta": bf(np.random.random((K, N)) * 1.7 / np.sqrt(K) / s[:, None]),
            "bias_lin": bf(np.random.standard_normal(N) * 0.1),
            "W1": bf(-np.random.random((NH, K)) * 1.7 / np.sqrt(K) / s[None, :]),
            "W2": bf(np.random.random((N, NH)) * (0.5 + np.random.random((N, 1))) * 2.0 / NH**2),
            "bias1": bf(np.random.standard_normal(NH) * 0.1),
            "bias2": bf(np.random.standard_normal(N) * 0.1),
            "adv": 1}


def reference(x, y, beta, bias_lin, W1, W2, bias1, bias2, adv):
    xq = mxq(f64(x), 1, "e4m3")
    lin = (xq @ mxq(f64(beta), 0, "e4m3")) + f64(bias_lin)
    if adv:
        beta_norm = np.sum(np.abs(f64(beta)), axis=0)
        lin = lin - EPSILON * f64(y) * beta_norm
    if adv:
        one = NH * np.sum(f64(W2), axis=1) + f64(bias2)
        one = np.broadcast_to(one, lin.shape)
    else:
        h = np.maximum((xq @ mxq(f64(W1), 1, "e4m3").T) + f64(bias1), 0.0)
        one = (mxq(h, 1, "e4m3") @ mxq(f64(W2), 1, "e4m3").T) + f64(bias2)
    return lin + one

@@ -1,0 +1,208 @@
+from contextlib import ExitStack
+
+import concourse.mybir as mybir
+from concourse.masks import make_identity
+
+F32 = mybir.dt.float32
+BF16 = mybir.dt.bfloat16
+U32 = mybir.dt.uint32
+U8 = mybir.dt.uint8
+FP8X4 = mybir.dt.float8_e4m3fn_x4
+ADD = mybir.AluOpType.add
+MULT = mybir.AluOpType.mult
+ACT = mybir.ActivationFunctionType
+
+P = 128
+B, K, N, NH = 8192, 1024, 128, 512
+NT = B // P
+GT = 4
+NG = NT // GT
+FLOPS = 2 * B * K * N
+BYTES = 2 * (B * K + B * N + K * N + N * NH + 2 * N) + 4 * B * N
+
+PIN = False
+X_CHUNKS = [4,4,8,8,8,8,8,8,4,4]
+Y_CHUNKS = [16,16,16,16]
+O_CHUNKS = [8,8,8,8,8,8,8,4,4]
+GP_MUL = True
+VCOPY = [[]]
+GRP_BUFS = 3
+XT_BUFS = 6
+STORE_Q = "sync"
+
+
+def starts(chunks):
+    res = []
+    s = 0
+    for c in chunks:
+        res.append(s)
+        s += c
+    assert s == NT
+    return res
+
+
+def tile_advresnet_t_kernel(tc, x, y, beta, bias_lin, W1, W2, bias1, bias2, adv, out):
+    assert adv == 1
+    nc = tc.nc
+    with ExitStack() as ctx:
+        if PIN:
+            ctx.enter_context(tc.manual_schedule())
+        res = ctx.enter_context(tc.tile_pool(name="res", bufs=1))
+        grp_pool = ctx.enter_context(tc.tile_pool(name="grp", bufs=GRP_BUFS))
+        cod_pool = ctx.enter_context(tc.tile_pool(name="cod", bufs=2))
+        ps_x = ctx.enter_context(tc.psum_pool(name="psx", bufs=XT_BUFS))
+        ps_o = ctx.enter_context(tc.psum_pool(name="pso", bufs=8 - XT_BUFS))
+
+        x_v = x.rearrange("(p t) k -> p t k", t=NT)
+        y_v = y.rearrange("(p t) j -> p t j", t=NT)
+        o_v = out.rearrange("(p t) j -> p t j", t=NT)
+
+        ident = res.tile([P, P], F32, name="ident")
+        make_identity(nc, ident[:])
+        ones = res.tile([P, P], F32, name="ones")
+        nc.vector.memset(ones[:], 1.0)
+        brows = res.tile([P, N], BF16, name="brows")
+        nc.vector.memset(brows[:], 0.0)
+
+        braw = res.tile([P, 8 * N], BF16, name="braw")
+        nc.scalar.dma_start(
+            out=braw[:].rearrange("p (w c) -> p w c", w=4),
+            in_=beta.rearrange("(w p e) j -> p w (e j)", w=4, p=P, e=2),
+        )
+        w2 = res.tile([P, NH], BF16, name="w2")
+        nc.scalar.dma_start(out=w2[:], in_=W2)
+        nc.scalar.dma_start(out=brows[0:1, :], in_=bias_lin.rearrange("(o n) -> o n", o=1))
+        nc.scalar.dma_start(out=brows[1:2, :], in_=bias2.rearrange("(o n) -> o n", o=1))
+
+        x_st = starts(X_CHUNKS)
+        y_st = starts(Y_CHUNKS)
+        o_st = starts(O_CHUNKS)
+        x_tiles = []
+        y_tiles = []
+        yi = 0
+        for i, c in enumerate(X_CHUNKS):
+            xt_sb = res.tile([P, c * K], BF16, name="x%d" % i)
+            nc.sync.dma_start(out=xt_sb[:], in_=x_v[:, x_st[i] : x_st[i] + c, :].rearrange("p t k -> p (t k)"))
+            x_tiles.append(xt_sb)
+            while yi < len(Y_CHUNKS) and y_st[yi] < x_st[i] + c:
+                yc = Y_CHUNKS[yi]
+                y_sb = res.tile([P, yc * N], BF16, name="y%d" % yi)
+                nc.sync.dma_start(out=y_sb[:], in_=y_v[:, y_st[yi] : y_st[yi] + yc, :].rearrange("p t j -> p (t j)"))
+                y_tiles.append(y_sb)
+                yi += 1
+
+        def find(st, chunks, t):
+            for i, s in enumerate(st):
+                if s <= t < s + chunks[i]:
+                    return i, t - s
+            raise ValueError("tile out of range")
+
+        bgrp = res.tile([P, 8 * N], BF16, name="bgrp", align_bytes=64)
+        nc.vector.tensor_copy(
+            out=bgrp[:].rearrange("p (g j t) -> p g j t", g=2, t=4),
+            in_=braw[:].rearrange("p (g t j) -> p g j t", g=2, t=4),
+        )
+        absb = res.tile([P, 8 * N], F32, name="absb")
+        nc.scalar.activation(out=absb[:], in_=braw[:], func=ACT.Abs)
+        w2junk = res.tile([P, NH], F32, name="w2junk")
+        w2s = res.tile([P, 1], F32, name="w2s")
+        nc.scalar.activation(out=w2junk[:], in_=w2[:], func=ACT.Copy, scale=float(NH), accum_out=w2s[:])
+        rhs_c = res.tile([P, 2 * N], F32, name="rhs_c")
+        nc.vector.tensor_reduce(
+            out=rhs_c[:, 0:N], in_=absb[:].rearrange("p (a j) -> p j a", a=8), axis=mybir.AxisListType.X, op=ADD
+        )
+        bcod = res.tile([P, 2 * N], U32, name="bcod", align_bytes=64)
+        bscl = res.tile([P, 2 * N], U8, name="bscl", align_bytes=64)
+        nc.vector.quantize_mx(out=bcod[:].bitcast(FP8X4), scales=bscl[:], in_=bgrp[:])
+        nc.vector.scalar_tensor_tensor(
+            out=rhs_c[:, N : 2 * N], in0=ident[:], scalar=w2s[:, 0:1], in1=brows[:], op0=MULT, op1=ADD
+        )
+        sc = res.tile([P, 2 * N], F32, name="sc")
+
+        def emit_consts():
+            sc_ps = ps_o.tile([P, GT * N], F32, name="ops")
+            nc.tensor.matmul(out=sc_ps[:, 0 : 2 * N], lhsT=ones[:], rhs=rhs_c[:], start=True, stop=True)
+            nc.vector.tensor_scalar_mul(out=sc[:, 0:N], in0=sc_ps[:, 0:N], scalar1=-0.1)
+            nc.vector.tensor_copy(out=sc[:, N : 2 * N], in_=sc_ps[:, N : 2 * N])
+
+        grp_t = {}
+        cod_t = {}
+        ops_t = {}
+        o_tiles = {}
+
+        def emit_transposes(g):
+            grp = grp_pool.tile([P, GT * K], BF16, name="grp", align_bytes=64)
+            grp_t[g] = grp
+            for tt in range(GT):
+                t = g * GT + tt
+                i, r = find(x_st, X_CHUNKS, t)
+                xw = x_tiles[i][:, r * K : (r + 1) * K].bitcast(F32)
+                xt = ps_x.tile([P, 4, P], F32, name="xt")
+                for w in range(4):
+                    nc.tensor.transpose(xt[:, w, :], xw[:, w * P : (w + 1) * P], ident[:])
+                dst = grp[:, tt * K : (tt + 1) * K].bitcast(F32).rearrange("p (g r u) -> p g r u", g=2, u=2)
+                src = xt[:].rearrange("p (g u) r -> p g r u", u=2)
+                if tt in VCOPY[g % len(VCOPY)]:
+                    nc.vector.tensor_copy(out=dst, in_=src)
+                else:
+                    nc.scalar.copy(out=dst, in_=src)
+
+        def emit_quant(g):
+            cod = cod_pool.tile([P, GT * 2 * P], U32, name="cod", align_bytes=64)
+            scl = cod_pool.tile([P, GT * 2 * P], U8, name="scl", align_bytes=64)
+            cod_t[g] = (cod, scl)
+            nc.vector.quantize_mx(out=cod[:].bitcast(FP8X4), scales=scl[:], in_=grp_t[g][:])
+
+        def emit_mx(g):
+            cod, scl = cod_t[g]
+            ops = ps_o.tile([P, GT * N], F32, name="ops")
+            ops_t[g] = ops
+            for tt in range(GT):
+                for h in range(2):
+                    cs = slice((2 * tt + h) * P, (2 * tt + h + 1) * P)
+                    nc.tensor.matmul_mx(
+                        out=ops[:, tt * N : (tt + 1) * N],
+                        lhsT=cod[:, cs].bitcast(FP8X4),
+                        lhsT_scale=scl[:, cs],
+                        rhs=bcod[:, h * N : (h + 1) * N].bitcast(FP8X4),
+                        rhs_scale=bscl[:, h * N : (h + 1) * N],
+                        start=(h == 0),
+                        stop=(h == 1),
+                    )
+
+        def emit_yterm(ci):
+            c = O_CHUNKS[ci]
+            o_sb = res.tile([P, c * N], F32, name="o%d" % ci)
+            o_tiles[ci] = o_sb
+            i, r = find(y_st, Y_CHUNKS, o_st[ci])
+            y3 = y_tiles[i][:, r * N : (r + c) * N].rearrange("p (t j) -> p t j", j=N)
+            o3 = o_sb[:].rearrange("p (t j) -> p t j", j=N)
+            eng = nc.gpsimd if GP_MUL else nc.vector
+            eng.tensor_tensor(out=o3, in0=y3, in1=sc[:, 0:N].unsqueeze(1).to_broadcast([P, c, N]), op=MULT)
+            nc.vector.tensor_tensor(out=o3, in0=o3, in1=sc[:, N : 2 * N].unsqueeze(1).to_broadcast([P, c, N]), op=ADD)
+
+        def emit_epilogue(g):
+            ci, r = find(o_st, O_CHUNKS, g * GT)
+            o_sb = o_tiles[ci]
+            cols = slice(r * N, (r + GT) * N)
+            nc.vector.tensor_tensor(out=o_sb[:, cols], in0=ops_t[g][:], in1=o_sb[:, cols], op=ADD)
+            if r + GT == O_CHUNKS[ci]:
+                q = nc.sync if STORE_Q == "sync" else nc.gpsimd
+                q.dma_start(
+                    out=o_v[:, o_st[ci] : o_st[ci] + O_CHUNKS[ci], :].rearrange("p t j -> p (t j)"), in_=o_sb[:]
+                )
+
+        for g in range(NG + 2):
+            if g < NG:
+                emit_transposes(g)
+            if g == 1:
+                emit_consts()
+            if 1 <= g <= NG:
+                emit_quant(g - 1)
+                emit_mx(g - 1)
+            if g >= 1:
+                for ci, s in enumerate(o_st):
+                    if s == (g - 1) * GT:
+                        emit_yterm(ci)
+            if g >= 2:
+                emit_epilogue(g - 2)

@@ -20,11 +20,11 @@ NG = NT // GT
 FLOPS = 2 * B * K * N
 BYTES = 2 * (B * K + B * N + K * N + N * NH + 2 * N) + 4 * B * N
 
-PIN = False
+PIN = True
 X_CHUNKS = [4,4,8,8,8,8,8,8,4,4]
 Y_CHUNKS = [16,16,16,16]
 O_CHUNKS = [8,8,8,8,8,8,8,4,4]
-GP_MUL = True
+GP_MUL = False
 VCOPY = [[]]
 GRP_BUFS = 3
 XT_BUFS = 6

@@ -17,28 +17,23 @@ B, K, N, NH = 8192, 1024, 128, 512
 NT = B // P
 GT = 4
 NG = NT // GT
+CT = 8
+NC = NT // CT
 FLOPS = 2 * B * K * N
 BYTES = 2 * (B * K + B * N + K * N + N * NH + 2 * N) + 4 * B * N
 
 PIN = True
-X_CHUNKS = [4,4,8,8,8,8,8,8,4,4]
-Y_CHUNKS = [16,16,16,16]
-O_CHUNKS = [8,8,8,8,8,8,8,4,4]
-GP_MUL = False
-VCOPY = [[]]
+X_CHUNKS = [4,4,4,4,8,8,8,8,8,4,4]
+Y_BEFORE = [0,2,5,7]
+LAG_Q, LAG_M, LAG_E = 2, 3, 4
+Y_HEAD = 3
+G_CHUNKS = []
+G_SPLIT = 4
+VCOPY = []
 GRP_BUFS = 3
+COD_BUFS = 3
 XT_BUFS = 6
-STORE_Q = "sync"
-
-
-def starts(chunks):
-    res = []
-    s = 0
-    for c in chunks:
-        res.append(s)
-        s += c
-    assert s == NT
-    return res
+LAST_Q_SPLIT = False
 
 
 def tile_advresnet_t_kernel(tc, x, y, beta, bias_lin, W1, W2, bias1, bias2, adv, out):
@@ -49,20 +44,13 @@ def tile_advresnet_t_kernel(tc, x, y, beta, bias_lin, W1, W2, bias1, bias2, adv,
             ctx.enter_context(tc.manual_schedule())
         res = ctx.enter_context(tc.tile_pool(name="res", bufs=1))
         grp_pool = ctx.enter_context(tc.tile_pool(name="grp", bufs=GRP_BUFS))
-        cod_pool = ctx.enter_context(tc.tile_pool(name="cod", bufs=2))
+        cod_pool = ctx.enter_context(tc.tile_pool(name="cod", bufs=COD_BUFS))
         ps_x = ctx.enter_context(tc.psum_pool(name="psx", bufs=XT_BUFS))
         ps_o = ctx.enter_context(tc.psum_pool(name="pso", bufs=8 - XT_BUFS))
 
         x_v = x.rearrange("(p t) k -> p t k", t=NT)
         y_v = y.rearrange("(p t) j -> p t j", t=NT)
         o_v = out.rearrange("(p t) j -> p t j", t=NT)
-
-        ident = res.tile([P, P], F32, name="ident")
-        make_identity(nc, ident[:])
-        ones = res.tile([P, P], F32, name="ones")
-        nc.vector.memset(ones[:], 1.0)
-        brows = res.tile([P, N], BF16, name="brows")
-        nc.vector.memset(brows[:], 0.0)
 
         braw = res.tile([P, 8 * N], BF16, name="braw")
         nc.scalar.dma_start(
@@ -71,78 +59,84 @@ def tile_advresnet_t_kernel(tc, x, y, beta, bias_lin, W1, W2, bias1, bias2, adv,
         )
         w2 = res.tile([P, NH], BF16, name="w2")
         nc.scalar.dma_start(out=w2[:], in_=W2)
+        brows = res.tile([P, N], BF16, name="brows")
+        nc.vector.memset(brows[:], 0.0)
         nc.scalar.dma_start(out=brows[0:1, :], in_=bias_lin.rearrange("(o n) -> o n", o=1))
         nc.scalar.dma_start(out=brows[1:2, :], in_=bias2.rearrange("(o n) -> o n", o=1))
 
-        x_st = starts(X_CHUNKS)
-        y_st = starts(Y_CHUNKS)
-        o_st = starts(O_CHUNKS)
         x_tiles = []
+        x_of = []
         y_tiles = []
-        yi = 0
+        s = 0
         for i, c in enumerate(X_CHUNKS):
-            xt_sb = res.tile([P, c * K], BF16, name="x%d" % i)
-            nc.sync.dma_start(out=xt_sb[:], in_=x_v[:, x_st[i] : x_st[i] + c, :].rearrange("p t k -> p (t k)"))
-            x_tiles.append(xt_sb)
-            while yi < len(Y_CHUNKS) and y_st[yi] < x_st[i] + c:
-                yc = Y_CHUNKS[yi]
-                y_sb = res.tile([P, yc * N], BF16, name="y%d" % yi)
-                nc.sync.dma_start(out=y_sb[:], in_=y_v[:, y_st[yi] : y_st[yi] + yc, :].rearrange("p t j -> p (t j)"))
-                y_tiles.append(y_sb)
-                yi += 1
+            for yi, b in enumerate(Y_BEFORE):
+                if b == i:
+                    y_sb = res.tile([P, 16 * N], BF16, name="y%d" % yi)
+                    nc.sync.dma_start(out=y_sb[:], in_=y_v[:, 16 * yi : 16 * yi + 16, :].rearrange("p t j -> p (t j)"))
+                    y_tiles.append(y_sb)
+            x_sb = res.tile([P, c * K], BF16, name="x%d" % i)
+            nc.sync.dma_start(out=x_sb[:], in_=x_v[:, s : s + c, :].rearrange("p t k -> p (t k)"))
+            x_tiles.append(x_sb)
+            for r in range(c):
+                x_of.append((i, r))
+            s += c
+        assert s == NT
 
-        def find(st, chunks, t):
-            for i, s in enumerate(st):
-                if s <= t < s + chunks[i]:
-                    return i, t - s
-            raise ValueError("tile out of range")
+        ident = res.tile([P, P], F32, name="ident")
+        make_identity(nc, ident[:])
+        ones_f = res.tile([P, P], F32, name="ones_f")
+        nc.vector.memset(ones_f[:], 1.0)
+        ones_b = res.tile([P, P], BF16, name="ones_b")
+        nc.vector.memset(ones_b[:], 1.0)
+        warm = res.tile([P, 1], F32, name="warm")
+        nc.vector.memset(warm[:], 0.0)
+        nc.scalar.activation(out=warm[:], in_=warm[:], func=ACT.Abs)
 
         bgrp = res.tile([P, 8 * N], BF16, name="bgrp", align_bytes=64)
         nc.vector.tensor_copy(
             out=bgrp[:].rearrange("p (g j t) -> p g j t", g=2, t=4),
             in_=braw[:].rearrange("p (g t j) -> p g j t", g=2, t=4),
         )
-        absb = res.tile([P, 8 * N], F32, name="absb")
+        absb = res.tile([P, 8 * N], BF16, name="absb")
         nc.scalar.activation(out=absb[:], in_=braw[:], func=ACT.Abs)
         w2junk = res.tile([P, NH], F32, name="w2junk")
         w2s = res.tile([P, 1], F32, name="w2s")
         nc.scalar.activation(out=w2junk[:], in_=w2[:], func=ACT.Copy, scale=float(NH), accum_out=w2s[:])
-        rhs_c = res.tile([P, 2 * N], F32, name="rhs_c")
-        nc.vector.tensor_reduce(
-            out=rhs_c[:, 0:N], in_=absb[:].rearrange("p (a j) -> p j a", a=8), axis=mybir.AxisListType.X, op=ADD
-        )
         bcod = res.tile([P, 2 * N], U32, name="bcod", align_bytes=64)
         bscl = res.tile([P, 2 * N], U8, name="bscl", align_bytes=64)
         nc.vector.quantize_mx(out=bcod[:].bitcast(FP8X4), scales=bscl[:], in_=bgrp[:])
+        rhs_c = res.tile([P, N], F32, name="rhs_c")
         nc.vector.scalar_tensor_tensor(
-            out=rhs_c[:, N : 2 * N], in0=ident[:], scalar=w2s[:, 0:1], in1=brows[:], op0=MULT, op1=ADD
+            out=rhs_c[:], in0=ident[:], scalar=w2s[:, 0:1], in1=brows[:], op0=MULT, op1=ADD
         )
         sc = res.tile([P, 2 * N], F32, name="sc")
-
-        def emit_consts():
-            sc_ps = ps_o.tile([P, GT * N], F32, name="ops")
-            nc.tensor.matmul(out=sc_ps[:, 0 : 2 * N], lhsT=ones[:], rhs=rhs_c[:], start=True, stop=True)
-            nc.vector.tensor_scalar_mul(out=sc[:, 0:N], in0=sc_ps[:, 0:N], scalar1=-0.1)
-            nc.vector.tensor_copy(out=sc[:, N : 2 * N], in_=sc_ps[:, N : 2 * N])
+        sc_ps = ps_o.tile([P, GT * N], F32, name="ops")
+        for a in range(8):
+            nc.tensor.matmul(
+                out=sc_ps[:, 0:N], lhsT=ones_b[:], rhs=absb[:, a * N : (a + 1) * N], start=(a == 0), stop=(a == 7)
+            )
+        nc.tensor.matmul(out=sc_ps[:, N : 2 * N], lhsT=ones_f[:], rhs=rhs_c[:], start=True, stop=True)
+        nc.vector.tensor_scalar_mul(out=sc[:, 0:N], in0=sc_ps[:, 0:N], scalar1=-0.1)
+        nc.vector.tensor_copy(out=sc[:, N : 2 * N], in_=sc_ps[:, N : 2 * N])
 
         grp_t = {}
         cod_t = {}
         ops_t = {}
-        o_tiles = {}
+        o_tiles = [res.tile([P, CT * N], F32, name="o%d" % ci) for ci in range(NC)]
 
         def emit_transposes(g):
             grp = grp_pool.tile([P, GT * K], BF16, name="grp", align_bytes=64)
             grp_t[g] = grp
             for tt in range(GT):
                 t = g * GT + tt
-                i, r = find(x_st, X_CHUNKS, t)
+                i, r = x_of[t]
                 xw = x_tiles[i][:, r * K : (r + 1) * K].bitcast(F32)
                 xt = ps_x.tile([P, 4, P], F32, name="xt")
                 for w in range(4):
                     nc.tensor.transpose(xt[:, w, :], xw[:, w * P : (w + 1) * P], ident[:])
                 dst = grp[:, tt * K : (tt + 1) * K].bitcast(F32).rearrange("p (g r u) -> p g r u", g=2, u=2)
                 src = xt[:].rearrange("p (g u) r -> p g r u", u=2)
-                if tt in VCOPY[g % len(VCOPY)]:
+                if t in VCOPY:
                     nc.vector.tensor_copy(out=dst, in_=src)
                 else:
                     nc.scalar.copy(out=dst, in_=src)
@@ -151,7 +145,14 @@ def tile_advresnet_t_kernel(tc, x, y, beta, bias_lin, W1, W2, bias1, bias2, adv,
             cod = cod_pool.tile([P, GT * 2 * P], U32, name="cod", align_bytes=64)
             scl = cod_pool.tile([P, GT * 2 * P], U8, name="scl", align_bytes=64)
             cod_t[g] = (cod, scl)
-            nc.vector.quantize_mx(out=cod[:].bitcast(FP8X4), scales=scl[:], in_=grp_t[g][:])
+            parts = 2 if (LAST_Q_SPLIT and g == NG - 1) else 1
+            wq = GT * 2 * P // parts
+            for h in range(parts):
+                nc.vector.quantize_mx(
+                    out=cod[:, h * wq : (h + 1) * wq].bitcast(FP8X4),
+                    scales=scl[:, h * wq : (h + 1) * wq],
+                    in_=grp_t[g][:, 4 * h * wq : 4 * (h + 1) * wq],
+                )
 
         def emit_mx(g):
             cod, scl = cod_t[g]
@@ -170,39 +171,60 @@ def tile_advresnet_t_kernel(tc, x, y, beta, bias_lin, W1, W2, bias1, bias2, adv,
                         stop=(h == 1),
                     )
 
-        def emit_yterm(ci):
-            c = O_CHUNKS[ci]
-            o_sb = res.tile([P, c * N], F32, name="o%d" % ci)
-            o_tiles[ci] = o_sb
-            i, r = find(y_st, Y_CHUNKS, o_st[ci])
-            y3 = y_tiles[i][:, r * N : (r + c) * N].rearrange("p (t j) -> p t j", j=N)
-            o3 = o_sb[:].rearrange("p (t j) -> p t j", j=N)
-            eng = nc.gpsimd if GP_MUL else nc.vector
-            eng.tensor_tensor(out=o3, in0=y3, in1=sc[:, 0:N].unsqueeze(1).to_broadcast([P, c, N]), op=MULT)
-            nc.vector.tensor_tensor(out=o3, in0=o3, in1=sc[:, N : 2 * N].unsqueeze(1).to_broadcast([P, c, N]), op=ADD)
+        def emit_y(eng, step, ci, lo, hi):
+            n = hi - lo
+            o3 = o_tiles[ci][:, lo * N : hi * N].rearrange("p (t j) -> p t j", j=N)
+            if step == 0:
+                t0 = (ci % 2) * CT + lo
+                y3 = y_tiles[ci // 2][:, t0 * N : (t0 + n) * N].rearrange("p (t j) -> p t j", j=N)
+                eng.tensor_tensor(out=o3, in0=y3, in1=sc[:, 0:N].unsqueeze(1).to_broadcast([P, n, N]), op=MULT)
+            else:
+                eng.tensor_tensor(out=o3, in0=o3, in1=sc[:, N : 2 * N].unsqueeze(1).to_broadcast([P, n, N]), op=ADD)
 
         def emit_epilogue(g):
-            ci, r = find(o_st, O_CHUNKS, g * GT)
+            ci = g // 2
             o_sb = o_tiles[ci]
-            cols = slice(r * N, (r + GT) * N)
+            cols = slice((g % 2) * GT * N, (g % 2 + 1) * GT * N)
             nc.vector.tensor_tensor(out=o_sb[:, cols], in0=ops_t[g][:], in1=o_sb[:, cols], op=ADD)
-            if r + GT == O_CHUNKS[ci]:
-                q = nc.sync if STORE_Q == "sync" else nc.gpsimd
-                q.dma_start(
-                    out=o_v[:, o_st[ci] : o_st[ci] + O_CHUNKS[ci], :].rearrange("p t j -> p (t j)"), in_=o_sb[:]
-                )
+            if ci == NC - 1:
+                t0 = g * GT
+                nc.sync.dma_start(out=o_v[:, t0 : t0 + GT, :].rearrange("p t j -> p (t j)"), in_=o_sb[:, cols])
+            elif g % 2 == 1:
+                nc.sync.dma_start(out=o_v[:, ci * CT : (ci + 1) * CT, :].rearrange("p t j -> p (t j)"), in_=o_sb[:])
 
-        for g in range(NG + 2):
+        for ci in G_CHUNKS:
+            w = CT // G_SPLIT
+            for step in range(2):
+                for q in range(G_SPLIT):
+                    emit_y(nc.gpsimd, step, ci, q * w, (q + 1) * w)
+
+        v_chunks = [ci for ci in range(NC) if ci not in G_CHUNKS]
+        y_seq = []
+        for i in range(0, len(v_chunks), 2):
+            pair = v_chunks[i : i + 2]
+            for step in range(2):
+                for ci in pair:
+                    y_seq.append((step, ci))
+        y_done = []
+
+        def emit_next_y(k):
+            for unused in range(k):
+                if len(y_done) < len(y_seq):
+                    step, ci = y_seq[len(y_done)]
+                    emit_y(nc.vector, step, ci, 0, CT)
+                    y_done.append((step, ci))
+
+        emit_next_y(Y_HEAD)
+        for g in range(NG + LAG_E):
             if g < NG:
                 emit_transposes(g)
-            if g == 1:
-                emit_consts()
-            if 1 <= g <= NG:
-                emit_quant(g - 1)
-                emit_mx(g - 1)
-            if g >= 1:
-                for ci, s in enumerate(o_st):
-                    if s == (g - 1) * GT:
-                        emit_yterm(ci)
-            if g >= 2:
-                emit_epilogue(g - 2)
+            if 0 <= g - LAG_M < NG:
+                emit_mx(g - LAG_M)
+            if 0 <= g - LAG_Q < NG:
+                emit_quant(g - LAG_Q)
+            emit_next_y(1)
+            if 0 <= g - LAG_E < NG:
+                ci = (g - LAG_E) // 2
+                while ci not in G_CHUNKS and (1, ci) not in y_done:
+                    emit_next_y(1)
+                emit_epilogue(g - LAG_E)

@@ -17,46 +17,36 @@ B, K, N, NH = 8192, 1024, 128, 512
 NT = B // P
 GT = 4
 NG = NT // GT
-CT = 8
-NC = NT // CT
 FLOPS = 2 * B * K * N
 BYTES = 2 * (B * K + B * N + K * N + N * NH + 2 * N) + 4 * B * N
 
-PIN = True
-X_CHUNKS = [4,4,4,4,8,8,8,8,8,4,4]
-Y_BEFORE = [0,2,5,7]
-LAG_Q, LAG_M, LAG_E = 2, 3, 4
-Y_HEAD = 3
-G_CHUNKS = []
-G_SPLIT = 4
-VCOPY = []
+X_CHUNKS = [4,4,4,4,4,4,4,4,4,4,4,4,4,4,4,4]
+Y_BEFORE = [1,3,6,10]
+LAG_Q, LAG_M, LAG_E = 1, 2, 3
+Y_HEAD = 2
+ADD_ENGINE = "gpsimd"
 GRP_BUFS = 3
 COD_BUFS = 3
-XT_BUFS = 6
-LAST_Q_SPLIT = False
+XT_BUFS = 5
+LAST_Q_PARTS = 1
 
 
 def tile_advresnet_t_kernel(tc, x, y, beta, bias_lin, W1, W2, bias1, bias2, adv, out):
     assert adv == 1
     nc = tc.nc
     with ExitStack() as ctx:
-        if PIN:
-            ctx.enter_context(tc.manual_schedule())
+        ctx.enter_context(tc.manual_schedule())
         res = ctx.enter_context(tc.tile_pool(name="res", bufs=1))
         grp_pool = ctx.enter_context(tc.tile_pool(name="grp", bufs=GRP_BUFS))
         cod_pool = ctx.enter_context(tc.tile_pool(name="cod", bufs=COD_BUFS))
+        ps_c = ctx.enter_context(tc.psum_pool(name="psc", bufs=1))
         ps_x = ctx.enter_context(tc.psum_pool(name="psx", bufs=XT_BUFS))
-        ps_o = ctx.enter_context(tc.psum_pool(name="pso", bufs=8 - XT_BUFS))
+        ps_o = ctx.enter_context(tc.psum_pool(name="pso", bufs=7 - XT_BUFS))
 
         x_v = x.rearrange("(p t) k -> p t k", t=NT)
         y_v = y.rearrange("(p t) j -> p t j", t=NT)
         o_v = out.rearrange("(p t) j -> p t j", t=NT)
 
-        braw = res.tile([P, 8 * N], BF16, name="braw")
-        nc.scalar.dma_start(
-            out=braw[:].rearrange("p (w c) -> p w c", w=4),
-            in_=beta.rearrange("(w p e) j -> p w (e j)", w=4, p=P, e=2),
-        )
         w2 = res.tile([P, NH], BF16, name="w2")
         nc.scalar.dma_start(out=w2[:], in_=W2)
         brows = res.tile([P, N], BF16, name="brows")
@@ -64,6 +54,11 @@ def tile_advresnet_t_kernel(tc, x, y, beta, bias_lin, W1, W2, bias1, bias2, adv,
         nc.scalar.dma_start(out=brows[0:1, :], in_=bias_lin.rearrange("(o n) -> o n", o=1))
         nc.scalar.dma_start(out=brows[1:2, :], in_=bias2.rearrange("(o n) -> o n", o=1))
 
+        braw = res.tile([P, 8 * N], BF16, name="braw")
+        nc.sync.dma_start(
+            out=braw[:].rearrange("p (w c) -> p w c", w=4),
+            in_=beta.rearrange("(w p e) j -> p w (e j)", w=4, p=P, e=2),
+        )
         x_tiles = []
         x_of = []
         y_tiles = []
@@ -92,60 +87,60 @@ def tile_advresnet_t_kernel(tc, x, y, beta, bias_lin, W1, W2, bias1, bias2, adv,
         nc.vector.memset(warm[:], 0.0)
         nc.scalar.activation(out=warm[:], in_=warm[:], func=ACT.Abs)
 
-        bgrp = res.tile([P, 8 * N], BF16, name="bgrp", align_bytes=64)
-        nc.vector.tensor_copy(
-            out=bgrp[:].rearrange("p (g j t) -> p g j t", g=2, t=4),
-            in_=braw[:].rearrange("p (g t j) -> p g j t", g=2, t=4),
-        )
         absb = res.tile([P, 8 * N], BF16, name="absb")
         nc.scalar.activation(out=absb[:], in_=braw[:], func=ACT.Abs)
         w2junk = res.tile([P, NH], F32, name="w2junk")
         w2s = res.tile([P, 1], F32, name="w2s")
         nc.scalar.activation(out=w2junk[:], in_=w2[:], func=ACT.Copy, scale=float(NH), accum_out=w2s[:])
-        bcod = res.tile([P, 2 * N], U32, name="bcod", align_bytes=64)
-        bscl = res.tile([P, 2 * N], U8, name="bscl", align_bytes=64)
-        nc.vector.quantize_mx(out=bcod[:].bitcast(FP8X4), scales=bscl[:], in_=bgrp[:])
+        bgrp = res.tile([P, 8 * N], BF16, name="bgrp", align_bytes=64)
+        nc.vector.tensor_copy(
+            out=bgrp[:].rearrange("p (g j t) -> p g j t", g=2, t=4),
+            in_=braw[:].rearrange("p (g t j) -> p g j t", g=2, t=4),
+        )
         rhs_c = res.tile([P, N], F32, name="rhs_c")
         nc.vector.scalar_tensor_tensor(
             out=rhs_c[:], in0=ident[:], scalar=w2s[:, 0:1], in1=brows[:], op0=MULT, op1=ADD
         )
-        sc = res.tile([P, 2 * N], F32, name="sc")
-        sc_ps = ps_o.tile([P, GT * N], F32, name="ops")
+        cst = ps_c.tile([P, GT * N], F32, name="cst")
         for a in range(8):
             nc.tensor.matmul(
-                out=sc_ps[:, 0:N], lhsT=ones_b[:], rhs=absb[:, a * N : (a + 1) * N], start=(a == 0), stop=(a == 7)
+                out=cst[:, 0:N], lhsT=ones_b[:], rhs=absb[:, a * N : (a + 1) * N], start=(a == 0), stop=(a == 7)
             )
-        nc.tensor.matmul(out=sc_ps[:, N : 2 * N], lhsT=ones_f[:], rhs=rhs_c[:], start=True, stop=True)
-        nc.vector.tensor_scalar_mul(out=sc[:, 0:N], in0=sc_ps[:, 0:N], scalar1=-0.1)
-        nc.vector.tensor_copy(out=sc[:, N : 2 * N], in_=sc_ps[:, N : 2 * N])
+        c_sb = res.tile([P, N], F32, name="c_sb")
+
+        def emit_c():
+            c_ps = ps_o.tile([P, GT * N], F32, name="ops")
+            nc.tensor.matmul(out=c_ps[:, 0:N], lhsT=ones_f[:], rhs=rhs_c[:], start=True, stop=True)
+            nc.scalar.copy(out=c_sb[:], in_=c_ps[:, 0:N])
+
+        bcod = res.tile([P, 2 * N], U32, name="bcod", align_bytes=64)
+        bscl = res.tile([P, 2 * N], U8, name="bscl", align_bytes=64)
+        nc.vector.quantize_mx(out=bcod[:].bitcast(FP8X4), scales=bscl[:], in_=bgrp[:])
 
         grp_t = {}
         cod_t = {}
         ops_t = {}
-        o_tiles = [res.tile([P, CT * N], F32, name="o%d" % ci) for ci in range(NC)]
+        o_chunks = [res.tile([P, 2 * GT * N], F32, name="o%d" % ci) for ci in range(NG // 2)]
+        o_tiles = [o_chunks[g // 2][:, (g % 2) * GT * N : (g % 2 + 1) * GT * N] for g in range(NG)]
+        add_eng = nc.gpsimd if ADD_ENGINE == "gpsimd" else nc.vector
 
         def emit_transposes(g):
             grp = grp_pool.tile([P, GT * K], BF16, name="grp", align_bytes=64)
             grp_t[g] = grp
             for tt in range(GT):
-                t = g * GT + tt
-                i, r = x_of[t]
+                i, r = x_of[g * GT + tt]
                 xw = x_tiles[i][:, r * K : (r + 1) * K].bitcast(F32)
                 xt = ps_x.tile([P, 4, P], F32, name="xt")
                 for w in range(4):
                     nc.tensor.transpose(xt[:, w, :], xw[:, w * P : (w + 1) * P], ident[:])
                 dst = grp[:, tt * K : (tt + 1) * K].bitcast(F32).rearrange("p (g r u) -> p g r u", g=2, u=2)
-                src = xt[:].rearrange("p (g u) r -> p g r u", u=2)
-                if t in VCOPY:
-                    nc.vector.tensor_copy(out=dst, in_=src)
-                else:
-                    nc.scalar.copy(out=dst, in_=src)
+                nc.scalar.copy(out=dst, in_=xt[:].rearrange("p (g u) r -> p g r u", u=2))
 
         def emit_quant(g):
             cod = cod_pool.tile([P, GT * 2 * P], U32, name="cod", align_bytes=64)
             scl = cod_pool.tile([P, GT * 2 * P], U8, name="scl", align_bytes=64)
             cod_t[g] = (cod, scl)
-            parts = 2 if (LAST_Q_SPLIT and g == NG - 1) else 1
+            parts = LAST_Q_PARTS if g == NG - 1 else 1
             wq = GT * 2 * P // parts
             for h in range(parts):
                 nc.vector.quantize_mx(
@@ -171,60 +166,47 @@ def tile_advresnet_t_kernel(tc, x, y, beta, bias_lin, W1, W2, bias1, bias2, adv,
                         stop=(h == 1),
                     )
 
-        def emit_y(eng, step, ci, lo, hi):
-            n = hi - lo
-            o3 = o_tiles[ci][:, lo * N : hi * N].rearrange("p (t j) -> p t j", j=N)
-            if step == 0:
-                t0 = (ci % 2) * CT + lo
-                y3 = y_tiles[ci // 2][:, t0 * N : (t0 + n) * N].rearrange("p (t j) -> p t j", j=N)
-                eng.tensor_tensor(out=o3, in0=y3, in1=sc[:, 0:N].unsqueeze(1).to_broadcast([P, n, N]), op=MULT)
-            else:
-                eng.tensor_tensor(out=o3, in0=o3, in1=sc[:, N : 2 * N].unsqueeze(1).to_broadcast([P, n, N]), op=ADD)
+        def emit_y_mul(g):
+            t0 = (g % 4) * GT
+            nc.vector.scalar_tensor_tensor(
+                out=o_tiles[g].rearrange("p (t j) -> p t j", j=N),
+                in0=y_tiles[g // 4][:, t0 * N : (t0 + GT) * N].rearrange("p (t j) -> p t j", j=N),
+                scalar=-0.1,
+                in1=cst[:, 0:N].unsqueeze(1).to_broadcast([P, GT, N]),
+                op0=MULT,
+                op1=MULT,
+            )
+
+        def emit_y_add(g):
+            o3 = o_tiles[g].rearrange("p (t j) -> p t j", j=N)
+            add_eng.tensor_tensor(out=o3, in0=o3, in1=c_sb[:].unsqueeze(1).to_broadcast([P, GT, N]), op=ADD)
 
         def emit_epilogue(g):
-            ci = g // 2
-            o_sb = o_tiles[ci]
-            cols = slice((g % 2) * GT * N, (g % 2 + 1) * GT * N)
-            nc.vector.tensor_tensor(out=o_sb[:, cols], in0=ops_t[g][:], in1=o_sb[:, cols], op=ADD)
-            if ci == NC - 1:
-                t0 = g * GT
-                nc.sync.dma_start(out=o_v[:, t0 : t0 + GT, :].rearrange("p t j -> p (t j)"), in_=o_sb[:, cols])
+            nc.vector.tensor_tensor(out=o_tiles[g], in0=ops_t[g][:], in1=o_tiles[g], op=ADD)
+            if g >= NG - 2:
+                nc.sync.dma_start(out=o_v[:, g * GT : (g + 1) * GT, :].rearrange("p t j -> p (t j)"), in_=o_tiles[g])
             elif g % 2 == 1:
-                nc.sync.dma_start(out=o_v[:, ci * CT : (ci + 1) * CT, :].rearrange("p t j -> p (t j)"), in_=o_sb[:])
+                t0 = (g - 1) * GT
+                nc.sync.dma_start(
+                    out=o_v[:, t0 : t0 + 2 * GT, :].rearrange("p t j -> p (t j)"), in_=o_chunks[g // 2][:]
+                )
 
-        for ci in G_CHUNKS:
-            w = CT // G_SPLIT
-            for step in range(2):
-                for q in range(G_SPLIT):
-                    emit_y(nc.gpsimd, step, ci, q * w, (q + 1) * w)
-
-        v_chunks = [ci for ci in range(NC) if ci not in G_CHUNKS]
-        y_seq = []
-        for i in range(0, len(v_chunks), 2):
-            pair = v_chunks[i : i + 2]
-            for step in range(2):
-                for ci in pair:
-                    y_seq.append((step, ci))
-        y_done = []
-
-        def emit_next_y(k):
-            for unused in range(k):
-                if len(y_done) < len(y_seq):
-                    step, ci = y_seq[len(y_done)]
-                    emit_y(nc.vector, step, ci, 0, CT)
-                    y_done.append((step, ci))
-
-        emit_next_y(Y_HEAD)
+        for g in range(Y_HEAD):
+            emit_y_mul(g)
         for g in range(NG + LAG_E):
             if g < NG:
                 emit_transposes(g)
+            if g == 0:
+                emit_c()
+                for h in range(Y_HEAD):
+                    emit_y_add(h)
             if 0 <= g - LAG_M < NG:
                 emit_mx(g - LAG_M)
+            if 0 <= g - LAG_E < NG:
+                emit_epilogue(g - LAG_E)
+            if g + Y_HEAD < NG:
+                emit_y_mul(g + Y_HEAD)
             if 0 <= g - LAG_Q < NG:
                 emit_quant(g - LAG_Q)
-            emit_next_y(1)
-            if 0 <= g - LAG_E < NG:
-                ci = (g - LAG_E) // 2
-                while ci not in G_CHUNKS and (1, ci) not in y_done:
-                    emit_next_y(1)
-                emit_epilogue(g - LAG_E)
+            if g + Y_HEAD < NG:
+                emit_y_add(g + Y_HEAD)

@@ -21,7 +21,7 @@ FLOPS = 2 * B * K * N
 BYTES = 2 * (B * K + B * N + K * N + N * NH + 2 * N) + 4 * B * N
 
 X_CHUNKS = [4,4,4,4,4,4,4,4,4,4,4,4,4,4,4,4]
-Y_BEFORE = [1,3,6,10]
+Y_BEFORE = [0,2,6,10]
 LAG_Q, LAG_M, LAG_E = 1, 2, 3
 Y_HEAD = 2
 ADD_ENGINE = "gpsimd"

from contextlib import ExitStack

import concourse.mybir as mybir
from concourse.masks import make_identity

F32 = mybir.dt.float32
BF16 = mybir.dt.bfloat16
U32 = mybir.dt.uint32
U8 = mybir.dt.uint8
FP8X4 = mybir.dt.float8_e4m3fn_x4
ADD = mybir.AluOpType.add
MULT = mybir.AluOpType.mult
ACT = mybir.ActivationFunctionType

P = 128
B, K, N, NH = 8192, 1024, 128, 512
NT = B // P
GT = 4
NG = NT // GT
FLOPS = 2 * B * K * N
BYTES = 2 * (B * K + B * N + K * N + N * NH + 2 * N) + 4 * B * N

X_CHUNKS = [4,4,4,4,4,4,4,4,4,4,4,4,4,4,4,4]
Y_BEFORE = [0,2,6,10]
LAG_Q, LAG_M, LAG_E = 1, 2, 3
Y_HEAD = 2
ADD_ENGINE = "gpsimd"
GRP_BUFS = 3
COD_BUFS = 3
XT_BUFS = 5
LAST_Q_PARTS = 1


def tile_advresnet_t_kernel(tc, x, y, beta, bias_lin, W1, W2, bias1, bias2, adv, out):
    assert adv == 1
    nc = tc.nc
    with ExitStack() as ctx:
        ctx.enter_context(tc.manual_schedule())
        res = ctx.enter_context(tc.tile_pool(name="res", bufs=1))
        grp_pool = ctx.enter_context(tc.tile_pool(name="grp", bufs=GRP_BUFS))
        cod_pool = ctx.enter_context(tc.tile_pool(name="cod", bufs=COD_BUFS))
        ps_c = ctx.enter_context(tc.psum_pool(name="psc", bufs=1))
        ps_x = ctx.enter_context(tc.psum_pool(name="psx", bufs=XT_BUFS))
        ps_o = ctx.enter_context(tc.psum_pool(name="pso", bufs=7 - XT_BUFS))

        x_v = x.rearrange("(p t) k -> p t k", t=NT)
        y_v = y.rearrange("(p t) j -> p t j", t=NT)
        o_v = out.rearrange("(p t) j -> p t j", t=NT)

        w2 = res.tile([P, NH], BF16, name="w2")
        nc.scalar.dma_start(out=w2[:], in_=W2)
        brows = res.tile([P, N], BF16, name="brows")
        nc.vector.memset(brows[:], 0.0)
        nc.scalar.dma_start(out=brows[0:1, :], in_=bias_lin.rearrange("(o n) -> o n", o=1))
        nc.scalar.dma_start(out=brows[1:2, :], in_=bias2.rearrange("(o n) -> o n", o=1))

        braw = res.tile([P, 8 * N], BF16, name="braw")
        nc.sync.dma_start(
            out=braw[:].rearrange("p (w c) -> p w c", w=4),
            in_=beta.rearrange("(w p e) j -> p w (e j)", w=4, p=P, e=2),
        )
        x_tiles = []
        x_of = []
        y_tiles = []
        s = 0
        for i, c in enumerate(X_CHUNKS):
            for yi, b in enumerate(Y_BEFORE):
                if b == i:
                    y_sb = res.tile([P, 16 * N], BF16, name="y%d" % yi)
                    nc.sync.dma_start(out=y_sb[:], in_=y_v[:, 16 * yi : 16 * yi + 16, :].rearrange("p t j -> p (t j)"))
                    y_tiles.append(y_sb)
            x_sb = res.tile([P, c * K], BF16, name="x%d" % i)
            nc.sync.dma_start(out=x_sb[:], in_=x_v[:, s : s + c, :].rearrange("p t k -> p (t k)"))
            x_tiles.append(x_sb)
            for r in range(c):
                x_of.append((i, r))
            s += c
        assert s == NT

        ident = res.tile([P, P], F32, name="ident")
        make_identity(nc, ident[:])
        ones_f = res.tile([P, P], F32, name="ones_f")
        nc.vector.memset(ones_f[:], 1.0)
        ones_b = res.tile([P, P], BF16, name="ones_b")
        nc.vector.memset(ones_b[:], 1.0)
        warm = res.tile([P, 1], F32, name="warm")
        nc.vector.memset(warm[:], 0.0)
        nc.scalar.activation(out=warm[:], in_=warm[:], func=ACT.Abs)

        absb = res.tile([P, 8 * N], BF16, name="absb")
        nc.scalar.activation(out=absb[:], in_=braw[:], func=ACT.Abs)
        w2junk = res.tile([P, NH], F32, name="w2junk")
        w2s = res.tile([P, 1], F32, name="w2s")
        nc.scalar.activation(out=w2junk[:], in_=w2[:], func=ACT.Copy, scale=float(NH), accum_out=w2s[:])
        bgrp = res.tile([P, 8 * N], BF16, name="bgrp", align_bytes=64)
        nc.vector.tensor_copy(
            out=bgrp[:].rearrange("p (g j t) -> p g j t", g=2, t=4),
            in_=braw[:].rearrange("p (g t j) -> p g j t", g=2, t=4),
        )
        rhs_c = res.tile([P, N], F32, name="rhs_c")
        nc.vector.scalar_tensor_tensor(
            out=rhs_c[:], in0=ident[:], scalar=w2s[:, 0:1], in1=brows[:], op0=MULT, op1=ADD
        )
        cst = ps_c.tile([P, GT * N], F32, name="cst")
        for a in range(8):
            nc.tensor.matmul(
                out=cst[:, 0:N], lhsT=ones_b[:], rhs=absb[:, a * N : (a + 1) * N], start=(a == 0), stop=(a == 7)
            )
        c_sb = res.tile([P, N], F32, name="c_sb")

        def emit_c():
            c_ps = ps_o.tile([P, GT * N], F32, name="ops")
            nc.tensor.matmul(out=c_ps[:, 0:N], lhsT=ones_f[:], rhs=rhs_c[:], start=True, stop=True)
            nc.scalar.copy(out=c_sb[:], in_=c_ps[:, 0:N])

        bcod = res.tile([P, 2 * N], U32, name="bcod", align_bytes=64)
        bscl = res.tile([P, 2 * N], U8, name="bscl", align_bytes=64)
        nc.vector.quantize_mx(out=bcod[:].bitcast(FP8X4), scales=bscl[:], in_=bgrp[:])

        grp_t = {}
        cod_t = {}
        ops_t = {}
        o_chunks = [res.tile([P, 2 * GT * N], F32, name="o%d" % ci) for ci in range(NG // 2)]
        o_tiles = [o_chunks[g // 2][:, (g % 2) * GT * N : (g % 2 + 1) * GT * N] for g in range(NG)]
        add_eng = nc.gpsimd if ADD_ENGINE == "gpsimd" else nc.vector

        def emit_transposes(g):
            grp = grp_pool.tile([P, GT * K], BF16, name="grp", align_bytes=64)
            grp_t[g] = grp
            for tt in range(GT):
                i, r = x_of[g * GT + tt]
                xw = x_tiles[i][:, r * K : (r + 1) * K].bitcast(F32)
                xt = ps_x.tile([P, 4, P], F32, name="xt")
                for w in range(4):
                    nc.tensor.transpose(xt[:, w, :], xw[:, w * P : (w + 1) * P], ident[:])
                dst = grp[:, tt * K : (tt + 1) * K].bitcast(F32).rearrange("p (g r u) -> p g r u", g=2, u=2)
                nc.scalar.copy(out=dst, in_=xt[:].rearrange("p (g u) r -> p g r u", u=2))

        def emit_quant(g):
            cod = cod_pool.tile([P, GT * 2 * P], U32, name="cod", align_bytes=64)
            scl = cod_pool.tile([P, GT * 2 * P], U8, name="scl", align_bytes=64)
            cod_t[g] = (cod, scl)
            parts = LAST_Q_PARTS if g == NG - 1 else 1
            wq = GT * 2 * P // parts
            for h in range(parts):
                nc.vector.quantize_mx(
                    out=cod[:, h * wq : (h + 1) * wq].bitcast(FP8X4),
                    scales=scl[:, h * wq : (h + 1) * wq],
                    in_=grp_t[g][:, 4 * h * wq : 4 * (h + 1) * wq],
                )

        def emit_mx(g):
            cod, scl = cod_t[g]
            ops = ps_o.tile([P, GT * N], F32, name="ops")
            ops_t[g] = ops
            for tt in range(GT):
                for h in range(2):
                    cs = slice((2 * tt + h) * P, (2 * tt + h + 1) * P)
                    nc.tensor.matmul_mx(
                        out=ops[:, tt * N : (tt + 1) * N],
                        lhsT=cod[:, cs].bitcast(FP8X4),
                        lhsT_scale=scl[:, cs],
                        rhs=bcod[:, h * N : (h + 1) * N].bitcast(FP8X4),
                        rhs_scale=bscl[:, h * N : (h + 1) * N],
                        start=(h == 0),
                        stop=(h == 1),
                    )

        def emit_y_mul(g):
            t0 = (g % 4) * GT
            nc.vector.scalar_tensor_tensor(
                out=o_tiles[g].rearrange("p (t j) -> p t j", j=N),
                in0=y_tiles[g // 4][:, t0 * N : (t0 + GT) * N].rearrange("p (t j) -> p t j", j=N),
                scalar=-0.1,
                in1=cst[:, 0:N].unsqueeze(1).to_broadcast([P, GT, N]),
                op0=MULT,
                op1=MULT,
            )

        def emit_y_add(g):
            o3 = o_tiles[g].rearrange("p (t j) -> p t j", j=N)
            add_eng.tensor_tensor(out=o3, in0=o3, in1=c_sb[:].unsqueeze(1).to_broadcast([P, GT, N]), op=ADD)

        def emit_epilogue(g):
            nc.vector.tensor_tensor(out=o_tiles[g], in0=ops_t[g][:], in1=o_tiles[g], op=ADD)
            if g >= NG - 2:
                nc.sync.dma_start(out=o_v[:, g * GT : (g + 1) * GT, :].rearrange("p t j -> p (t j)"), in_=o_tiles[g])
            elif g % 2 == 1:
                t0 = (g - 1) * GT
                nc.sync.dma_start(
                    out=o_v[:, t0 : t0 + 2 * GT, :].rearrange("p t j -> p (t j)"), in_=o_chunks[g // 2][:]
                )

        for g in range(Y_HEAD):
            emit_y_mul(g)
        for g in range(NG + LAG_E):
            if g < NG:
                emit_transposes(g)
            if g == 0:
                emit_c()
                for h in range(Y_HEAD):
                    emit_y_add(h)
            if 0 <= g - LAG_M < NG:
                emit_mx(g - LAG_M)
            if 0 <= g - LAG_E < NG:
                emit_epilogue(g - LAG_E)
            if g + Y_HEAD < NG:
                emit_y_mul(g + Y_HEAD)
            if 0 <= g - LAG_Q < NG:
                emit_quant(g - LAG_Q)
            if g + Y_HEAD < NG:
                emit_y_add(g + Y_HEAD)
